import numpy as np
import ml_dtypes


def mxq(x, axis, fmt="e4m3"):
    dtype, down = {"e4m3": (ml_dtypes.float8_e4m3fn, 7), "e5m2": (ml_dtypes.float8_e5m2, 14)}[fmt]
    v = np.moveaxis(np.asarray(x, np.float32).astype(ml_dtypes.bfloat16).astype(np.float64), axis, -1)
    blocks = v.reshape(v.shape[:-1] + (-1, 32))
    amax = np.abs(blocks).max(-1, keepdims=True)
    byte = np.maximum(np.where(amax > 0, np.frexp(amax)[1] - 1 + 127, 0) - down, 1)
    scale = np.exp2(byte - 127.0)
    codes = (blocks / scale).astype(np.float32).astype(dtype).astype(np.float64)
    return np.moveaxis((codes * scale).reshape(v.shape), -1, axis)


WIDE = False


def mx_kscale(k):
    if not WIDE:
        return np.ones(k)
    levels = np.array([20, -20, 10, -10, 0])
    a = np.random.permutation(np.resize(levels, k // 512 * 4)).reshape(k // 512, 4)
    idx = np.arange(k)
    return np.exp2(a[idx // 512, idx % 128 // 32])


BF16 = ml_dtypes.bfloat16


def bf(x):
    return np.asarray(x, np.float32).astype(BF16)


def f64(x):
    return np.asarray(x).astype(np.float64)


B, Nb1, Nw1, Nb2x, Nb2y, Nw2x, Nw2y, R, C = 256, 2, 8, 4, 2, 16, 16, 1024, 2
J1 = Nb1 * Nb1
K1 = C * Nw1 * Nw1
J3 = Nb2x * Nb2y
L1 = J3 * R
J2 = J3 * J1


def setup_inputs():
    u = mx_kscale(L1)
    x = np.random.standard_normal((B, Nb1 * Nw1 * Nb1 * Nw1, C))
    k1 = np.random.standard_normal((J1, K1, L1)) / np.sqrt(K1) / u[None, None, :]
    b1 = np.random.standard_normal((1, J1, L1)) * 0.3
    gy = np.random.standard_normal((B, J1, J3, R)) * np.exp2(np.random.randint(-12, 1, (B, J1, 1, 1))) * 4.0
    gy = gy * u.reshape(J3, R)[None, None, :, :]
    g = gy.transpose(0, 3, 1, 2).reshape(B, J2, R)
    return {"x": bf(x), "k1": bf(k1), "b1": bf(b1), "grad_out": bf(g)}


def reference(x, k1, b1, grad_out):
    gy = f64(grad_out).reshape(B, R, J1, J3).transpose(2, 0, 3, 1).reshape(J1, B, L1)
    gh = mxq(gy, 2, "e5m2") @ mxq(f64(k1), 2, "e4m3").transpose(0, 2, 1)
    gh = gh.transpose(1, 0, 2).reshape(B, Nb1, Nb1, Nw1, Nw1, C).transpose(0, 1, 3, 2, 4, 5)
    return gh.reshape(B, Nb1 * Nw1 * Nb1 * Nw1, C)

@@ -1,0 +1,169 @@
+from contextlib import ExitStack
+
+import concourse.mybir as mybir
+from concourse.masks import make_identity
+
+F32 = mybir.dt.float32
+BF16 = mybir.dt.bfloat16
+I32 = mybir.dt.int32
+U32 = mybir.dt.uint32
+U8 = mybir.dt.uint8
+E4M3X4 = mybir.dt.float8_e4m3fn_x4
+E5M2X4 = mybir.dt.float8_e5m2_x4
+
+P = 128
+SAMPLES = 256
+BLOCKS = 4
+WINDOW = 128
+PLANES = 8
+R = 1024
+K_PASS = 512
+GROUPS = R // K_PASS
+PAIRS = PLANES // 2
+BANK = 512
+N_PASS = 512
+
+QUARTER = 64
+QUARTERS = SAMPLES // QUARTER
+HALF_RUN = (K_PASS // 2) * BLOCKS * PLANES
+FILLER = QUARTER
+GY_COLS = SAMPLES * 2 + FILLER
+
+FLOPS = 2 * SAMPLES * BLOCKS * WINDOW * PLANES * R
+BYTES = 2 * SAMPLES * BLOCKS * PLANES * R + 2 * BLOCKS * WINDOW * PLANES * R + 4 * SAMPLES * BLOCKS * WINDOW
+
+
+def tile_switchnet_fstar_pa_k_kernel(tc, x, k1, b1, grad_out, out):
+    nc = tc.nc
+    flat_grad = grad_out.rearrange("b a c -> b (a c)")
+    flat_out = out.rearrange("b g c -> b (g c)")
+
+    with ExitStack() as ctx:
+        keep = ctx.enter_context(tc.tile_pool(name="keep", bufs=1))
+        grad_pool = ctx.enter_context(tc.tile_pool(name="grad", bufs=5))
+        weight_pool = ctx.enter_context(tc.tile_pool(name="weight", bufs=4))
+        stage = ctx.enter_context(tc.tile_pool(name="stage", bufs=6))
+        result_pool = ctx.enter_context(tc.tile_pool(name="result", bufs=2))
+        sums = ctx.enter_context(tc.psum_pool(name="sums", bufs=1))
+        banks = ctx.enter_context(tc.psum_pool(name="banks", bufs=4))
+
+        ident = keep.tile([P, P], F32, name="ident")
+        make_identity(nc, ident[:])
+
+        k_codes = [keep.tile([P, 2 * PLANES * WINDOW], U32, name="k_codes%d" % j, align_bytes=64) for j in range(BLOCKS)]
+        k_scales = [keep.tile([P, 2 * PLANES * WINDOW], U8, name="k_scales%d" % j, align_bytes=64) for j in range(BLOCKS)]
+        gy_codes = [keep.tile([P, PAIRS, GY_COLS], U32, name="gy_codes%d" % j, align_bytes=64) for j in range(BLOCKS)]
+        gy_scales = [keep.tile([P, PAIRS, GY_COLS], U8, name="gy_scales%d" % j, align_bytes=64) for j in range(BLOCKS)]
+        acc = [sums.tile([P, N_PASS], F32, name="acc%d" % j) for j in range(BLOCKS)]
+
+        for j in range(BLOCKS):
+            nc.vector.memset(gy_codes[j][:, :, 2 * SAMPLES :].bitcast(I32), 0)
+            nc.vector.memset(gy_scales[j][:, :, 2 * SAMPLES :].bitcast(I32), 0)
+
+        def empty_bank(bank_no):
+            return nc.vector.tensor_copy if bank_no % 3 == 2 else nc.scalar.copy
+
+        def weights(j, first_bank_no):
+            for h in range(2):
+                raw = weight_pool.tile([P, PLANES * R // 2], BF16, name="raw")
+                nc.sync.dma_start(out=raw[:], in_=k1[j, :, h * (PLANES * R // 2) : (h + 1) * (PLANES * R // 2)])
+                words = raw[:].bitcast(F32)
+                for i in range(4):
+                    bank = banks.tile([P, BANK], F32, name="bank")
+                    for q in range(4):
+                        nc.tensor.transpose(
+                            bank[:, q * P : (q + 1) * P], words[:, i * BANK + q * P : i * BANK + (q + 1) * P], ident[:]
+                        )
+                    grouped = stage.tile([P, 2 * BANK], BF16, name="k_grouped", align_bytes=64)
+                    empty_bank(first_bank_no + 4 * h + i)(
+                        out=grouped[:].bitcast(F32).rearrange("p (c k u) -> p c k u", c=2, k=WINDOW, u=2),
+                        in_=bank[:].rearrange("p (c u k) -> p c k u", c=2, u=2, k=WINDOW),
+                    )
+                    cols = slice((8 * h + 2 * i) * WINDOW, (8 * h + 2 * i + 2) * WINDOW)
+                    nc.vector.quantize_mx(
+                        out=k_codes[j][:, cols].bitcast(E4M3X4), scales=k_scales[j][:, cols], in_=grouped[:]
+                    )
+
+        def load_grad(g, quarter):
+            rows = grad_pool.tile([P, HALF_RUN], BF16, name="rows")
+            for half in range(2):
+                nc.sync.dma_start(
+                    out=rows[half:P:2, :],
+                    in_=flat_grad[
+                        quarter * QUARTER : (quarter + 1) * QUARTER,
+                        (2 * g + half) * HALF_RUN : (2 * g + half + 1) * HALF_RUN,
+                    ],
+                )
+            return rows
+
+        def grad_block(rows, quarter, j, first_bank_no):
+            words = rows[:].bitcast(F32).rearrange("q (p w) -> q p w", w=32)
+            for i in range(2):
+                bank = banks.tile([P, BANK], F32, name="bank")
+                for uu in range(2):
+                    for odd in range(2):
+                        nc.tensor.transpose(
+                            bank[:, (2 * uu + odd) * P : (2 * uu + odd + 1) * P],
+                            words[:, :, odd * 16 + j * PAIRS + 2 * i + uu],
+                            ident[:],
+                        )
+                for uu in range(2):
+                    u = 2 * i + uu
+                    grouped = stage.tile([P, BANK], BF16, name="gy_grouped", align_bytes=64)
+                    empty_bank(first_bank_no + i)(
+                        out=grouped[:].rearrange("p (e q o) -> p e q o", e=2, q=P, o=2),
+                        in_=bank[:, uu * 2 * P : (uu + 1) * 2 * P].bitcast(BF16).rearrange("p (o q e) -> p e q o", o=2, q=P, e=2),
+                    )
+                    cols = slice(quarter * 2 * QUARTER, (quarter + 1) * 2 * QUARTER)
+                    nc.vector.quantize_mx(
+                        out=gy_codes[j][:, u, cols].bitcast(E5M2X4), scales=gy_scales[j][:, u, cols], in_=grouped[:]
+                    )
+
+        def multiply(g, j):
+            for u in range(PAIRS):
+                for e in range(2):
+                    k_cols = slice((2 * (2 * u + e) + g) * WINDOW, (2 * (2 * u + e) + g + 1) * WINDOW)
+                    gy_cols = slice(e * QUARTER, e * QUARTER + N_PASS)
+                    nc.tensor.matmul_mx(
+                        out=acc[j][:],
+                        lhsT=k_codes[j][:, k_cols].bitcast(E4M3X4),
+                        lhsT_scale=k_scales[j][:, k_cols],
+                        rhs=gy_codes[j][:, u, gy_cols].bitcast(E5M2X4),
+                        rhs_scale=gy_scales[j][:, u, gy_cols],
+                        start=(g == 0 and u == 0 and e == 0),
+                        stop=(g == GROUPS - 1 and u == PAIRS - 1 and e == 1),
+                    )
+
+        weights(0, 0)
+        for quarter in range(QUARTERS):
+            rows = load_grad(0, quarter)
+            for j in range(BLOCKS):
+                grad_block(rows, quarter, j, 2 * j)
+        multiply(0, 0)
+        for j in range(1, BLOCKS):
+            weights(j, 0)
+            multiply(0, j)
+        for quarter in range(QUARTERS):
+            rows = load_grad(1, quarter)
+            for j in range(BLOCKS):
+                grad_block(rows, quarter, j, 2 * j)
+                if quarter == QUARTERS - 1:
+                    multiply(1, j)
+
+        gh = [keep.tile([P, SAMPLES], F32, name="gh%d" % j) for j in range(BLOCKS)]
+        for j in range(BLOCKS):
+            empty_bank(j)(
+                out=gh[j][:].rearrange("k (q s) -> k q s", q=QUARTERS),
+                in_=acc[j][:].rearrange("k (q h s) -> k q h s", q=QUARTERS, h=2, s=QUARTER)[:, :, 0, :],
+            )
+        for half in range(SAMPLES // P):
+            bank = banks.tile([P, BANK], F32, name="bank")
+            for j in range(BLOCKS):
+                nc.tensor.transpose(bank[:, j * P : (j + 1) * P], gh[j][:, half * P : (half + 1) * P], ident[:])
+            grid = result_pool.tile([P, BANK], F32, name="grid")
+            for br in range(2):
+                empty_bank(half)(
+                    out=grid[:, br * 256 : (br + 1) * 256].rearrange("b (r c x) -> b r c x", r=8, c=2, x=16),
+                    in_=bank[:, br * 256 : (br + 1) * 256].rearrange("b (c r x) -> b r c x", c=2, r=8, x=16),
+                )
+            nc.sync.dma_start(out=flat_out[half * P : (half + 1) * P, :], in_=grid[:])

@@ -46,6 +46,7 @@ def tile_switchnet_fstar_pa_k_kernel(tc, x, k1, b1, grad_out, out):
         result_pool = ctx.enter_context(tc.tile_pool(name="result", bufs=2))
         sums = ctx.enter_context(tc.psum_pool(name="sums", bufs=1))
         banks = ctx.enter_context(tc.psum_pool(name="banks", bufs=4))
+        ctx.enter_context(tc.manual_schedule())
 
         ident = keep.tile([P, P], F32, name="ident")
         make_identity(nc, ident[:])
@@ -62,6 +63,13 @@ def tile_switchnet_fstar_pa_k_kernel(tc, x, k1, b1, grad_out, out):
 
         def empty_bank(bank_no):
             return nc.vector.tensor_copy if bank_no % 3 == 2 else nc.scalar.copy
+
+        held = {"calls": []}
+
+        def quantise_held():
+            for codes, scales, grouped in held["calls"]:
+                nc.vector.quantize_mx(out=codes, scales=scales, in_=grouped)
+            held["calls"] = []
 
         def weights(j, first_bank_no):
             for h in range(2):
@@ -80,9 +88,8 @@ def tile_switchnet_fstar_pa_k_kernel(tc, x, k1, b1, grad_out, out):
                         in_=bank[:].rearrange("p (c u k) -> p c k u", c=2, u=2, k=WINDOW),
                     )
                     cols = slice((8 * h + 2 * i) * WINDOW, (8 * h + 2 * i + 2) * WINDOW)
-                    nc.vector.quantize_mx(
-                        out=k_codes[j][:, cols].bitcast(E4M3X4), scales=k_scales[j][:, cols], in_=grouped[:]
-                    )
+                    quantise_held()
+                    held["calls"] = [(k_codes[j][:, cols].bitcast(E4M3X4), k_scales[j][:, cols], grouped[:])]
 
         def load_grad(g, quarter):
             rows = grad_pool.tile([P, HALF_RUN], BF16, name="rows")
@@ -107,6 +114,7 @@ def tile_switchnet_fstar_pa_k_kernel(tc, x, k1, b1, grad_out, out):
                             words[:, :, odd * 16 + j * PAIRS + 2 * i + uu],
                             ident[:],
                         )
+                copied = []
                 for uu in range(2):
                     u = 2 * i + uu
                     grouped = stage.tile([P, BANK], BF16, name="gy_grouped", align_bytes=64)
@@ -115,9 +123,9 @@ def tile_switchnet_fstar_pa_k_kernel(tc, x, k1, b1, grad_out, out):
                         in_=bank[:, uu * 2 * P : (uu + 1) * 2 * P].bitcast(BF16).rearrange("p (o q e) -> p e q o", o=2, q=P, e=2),
                     )
                     cols = slice(quarter * 2 * QUARTER, (quarter + 1) * 2 * QUARTER)
-                    nc.vector.quantize_mx(
-                        out=gy_codes[j][:, u, cols].bitcast(E5M2X4), scales=gy_scales[j][:, u, cols], in_=grouped[:]
-                    )
+                    copied.append((gy_codes[j][:, u, cols].bitcast(E5M2X4), gy_scales[j][:, u, cols], grouped[:]))
+                quantise_held()
+                held["calls"] = copied
 
         def multiply(g, j):
             for u in range(PAIRS):
@@ -139,16 +147,23 @@ def tile_switchnet_fstar_pa_k_kernel(tc, x, k1, b1, grad_out, out):
             rows = load_grad(0, quarter)
             for j in range(BLOCKS):
                 grad_block(rows, quarter, j, 2 * j)
-        multiply(0, 0)
         for j in range(1, BLOCKS):
             weights(j, 0)
-            multiply(0, j)
-        for quarter in range(QUARTERS):
+            multiply(0, j - 1)
+        for quarter in range(QUARTERS - 1):
             rows = load_grad(1, quarter)
             for j in range(BLOCKS):
                 grad_block(rows, quarter, j, 2 * j)
-                if quarter == QUARTERS - 1:
-                    multiply(1, j)
+                if quarter == 0 and j == 1:
+                    multiply(0, BLOCKS - 1)
+        rows = load_grad(1, QUARTERS - 1)
+        for j in range(BLOCKS):
+            grad_block(rows, QUARTERS - 1, j, 2 * j)
+            if j >= 2:
+                multiply(1, j - 2)
+        quantise_held()
+        multiply(1, BLOCKS - 2)
+        multiply(1, BLOCKS - 1)
 
         gh = [keep.tile([P, SAMPLES], F32, name="gh%d" % j) for j in range(BLOCKS)]
         for j in range(BLOCKS):

@@ -25,7 +25,10 @@ N_PASS = 512
 
 QUARTER = 64
 QUARTERS = SAMPLES // QUARTER
-HALF_RUN = (K_PASS // 2) * BLOCKS * PLANES
+PIECES = GROUPS * QUARTERS
+HALF_R = K_PASS // 2
+SWITCHED = BLOCKS * PLANES
+SORT = 4
 FILLER = QUARTER
 GY_COLS = SAMPLES * 2 + FILLER
 
@@ -40,9 +43,10 @@ def tile_switchnet_fstar_pa_k_kernel(tc, x, k1, b1, grad_out, out):
 
     with ExitStack() as ctx:
         keep = ctx.enter_context(tc.tile_pool(name="keep", bufs=1))
-        grad_pool = ctx.enter_context(tc.tile_pool(name="grad", bufs=5))
-        weight_pool = ctx.enter_context(tc.tile_pool(name="weight", bufs=4))
-        stage = ctx.enter_context(tc.tile_pool(name="stage", bufs=6))
+        grad_pool = ctx.enter_context(tc.tile_pool(name="grad", bufs=3))
+        sorted_pool = ctx.enter_context(tc.tile_pool(name="sorted", bufs=2))
+        weight_pool = ctx.enter_context(tc.tile_pool(name="weight", bufs=3))
+        stage = ctx.enter_context(tc.tile_pool(name="stage", bufs=8))
         result_pool = ctx.enter_context(tc.tile_pool(name="result", bufs=2))
         sums = ctx.enter_context(tc.psum_pool(name="sums", bufs=1))
         banks = ctx.enter_context(tc.psum_pool(name="banks", bufs=4))
@@ -61,20 +65,63 @@ def tile_switchnet_fstar_pa_k_kernel(tc, x, k1, b1, grad_out, out):
             nc.vector.memset(gy_codes[j][:, :, 2 * SAMPLES :].bitcast(I32), 0)
             nc.vector.memset(gy_scales[j][:, :, 2 * SAMPLES :].bitcast(I32), 0)
 
-        def empty_bank(bank_no):
-            return nc.vector.tensor_copy if bank_no % 3 == 2 else nc.scalar.copy
+        def load_grad(piece):
+            g, quarter = divmod(piece, QUARTERS)
+            rows = grad_pool.tile([P, HALF_R * SWITCHED], BF16, name="rows")
+            for half in range(2):
+                nc.sync.dma_start(
+                    out=rows[half:P:2, :],
+                    in_=flat_grad[
+                        quarter * QUARTER : (quarter + 1) * QUARTER,
+                        (2 * g + half) * HALF_R * SWITCHED : (2 * g + half + 1) * HALF_R * SWITCHED,
+                    ],
+                )
+            return rows
 
-        held = {"calls": []}
+        def undo_switch(rows):
+            by_r = rows[:].rearrange("q (r c) -> q r c", c=SWITCHED)
+            unswitched = sorted_pool.tile([P, SWITCHED, HALF_R], BF16, name="unswitched")
+            for c in range(0, SWITCHED, SORT):
+                nc.vector.tensor_copy(
+                    out=unswitched[:, c : c + SORT, :].rearrange("q c r -> q r c"), in_=by_r[:, :, c : c + SORT]
+                )
+            return unswitched
 
-        def quantise_held():
-            for codes, scales, grouped in held["calls"]:
-                nc.vector.quantize_mx(out=codes, scales=scales, in_=grouped)
-            held["calls"] = []
+        def transpose_grad(unswitched):
+            words = unswitched[:].bitcast(F32)
+            copied = []
+            for c in range(0, SWITCHED, 4):
+                bank = banks.tile([P, BANK], F32, name="bank")
+                for i in range(4):
+                    nc.tensor.transpose(bank[:, i * P : (i + 1) * P], words[:, c + i, :], ident[:])
+                grouped = stage.tile([P, 2 * BANK], BF16, name="gy_grouped", align_bytes=64)
+                nc.scalar.copy(out=grouped[:].bitcast(F32), in_=bank[:])
+                copied.append(grouped)
+            return copied
 
-        def weights(j, first_bank_no):
+        def quantise_grad(piece, j, copied):
+            quarter = piece % QUARTERS
+            cols = slice(quarter * 2 * QUARTER, (quarter + 1) * 2 * QUARTER)
+            for u in range(PAIRS):
+                grouped = copied[(j * PLANES + 2 * u) // 4]
+                first = (u % 2) * BANK
+                nc.vector.quantize_mx(
+                    out=gy_codes[j][:, u, cols].bitcast(E5M2X4),
+                    scales=gy_scales[j][:, u, cols],
+                    in_=grouped[:, first : first + BANK],
+                )
+
+        def load_weights(j):
+            raws = []
             for h in range(2):
                 raw = weight_pool.tile([P, PLANES * R // 2], BF16, name="raw")
                 nc.sync.dma_start(out=raw[:], in_=k1[j, :, h * (PLANES * R // 2) : (h + 1) * (PLANES * R // 2)])
+                raws.append(raw)
+            return raws
+
+        def transpose_weights(raws):
+            copied = []
+            for raw in raws:
                 words = raw[:].bitcast(F32)
                 for i in range(4):
                     bank = banks.tile([P, BANK], F32, name="bank")
@@ -83,49 +130,19 @@ def tile_switchnet_fstar_pa_k_kernel(tc, x, k1, b1, grad_out, out):
                             bank[:, q * P : (q + 1) * P], words[:, i * BANK + q * P : i * BANK + (q + 1) * P], ident[:]
                         )
                     grouped = stage.tile([P, 2 * BANK], BF16, name="k_grouped", align_bytes=64)
-                    empty_bank(first_bank_no + 4 * h + i)(
+                    nc.scalar.copy(
                         out=grouped[:].bitcast(F32).rearrange("p (c k u) -> p c k u", c=2, k=WINDOW, u=2),
                         in_=bank[:].rearrange("p (c u k) -> p c k u", c=2, u=2, k=WINDOW),
                     )
-                    cols = slice((8 * h + 2 * i) * WINDOW, (8 * h + 2 * i + 2) * WINDOW)
-                    quantise_held()
-                    held["calls"] = [(k_codes[j][:, cols].bitcast(E4M3X4), k_scales[j][:, cols], grouped[:])]
+                    copied.append(grouped)
+            return copied
 
-        def load_grad(g, quarter):
-            rows = grad_pool.tile([P, HALF_RUN], BF16, name="rows")
-            for half in range(2):
-                nc.sync.dma_start(
-                    out=rows[half:P:2, :],
-                    in_=flat_grad[
-                        quarter * QUARTER : (quarter + 1) * QUARTER,
-                        (2 * g + half) * HALF_RUN : (2 * g + half + 1) * HALF_RUN,
-                    ],
+        def quantise_weights(j, copied):
+            for i in range(len(copied)):
+                cols = slice(2 * i * WINDOW, (2 * i + 2) * WINDOW)
+                nc.vector.quantize_mx(
+                    out=k_codes[j][:, cols].bitcast(E4M3X4), scales=k_scales[j][:, cols], in_=copied[i][:]
                 )
-            return rows
-
-        def grad_block(rows, quarter, j, first_bank_no):
-            words = rows[:].bitcast(F32).rearrange("q (p w) -> q p w", w=32)
-            for i in range(2):
-                bank = banks.tile([P, BANK], F32, name="bank")
-                for uu in range(2):
-                    for odd in range(2):
-                        nc.tensor.transpose(
-                            bank[:, (2 * uu + odd) * P : (2 * uu + odd + 1) * P],
-                            words[:, :, odd * 16 + j * PAIRS + 2 * i + uu],
-                            ident[:],
-                        )
-                copied = []
-                for uu in range(2):
-                    u = 2 * i + uu
-                    grouped = stage.tile([P, BANK], BF16, name="gy_grouped", align_bytes=64)
-                    empty_bank(first_bank_no + i)(
-                        out=grouped[:].rearrange("p (e q o) -> p e q o", e=2, q=P, o=2),
-                        in_=bank[:, uu * 2 * P : (uu + 1) * 2 * P].bitcast(BF16).rearrange("p (o q e) -> p e q o", o=2, q=P, e=2),
-                    )
-                    cols = slice(quarter * 2 * QUARTER, (quarter + 1) * 2 * QUARTER)
-                    copied.append((gy_codes[j][:, u, cols].bitcast(E5M2X4), gy_scales[j][:, u, cols], grouped[:]))
-                quantise_held()
-                held["calls"] = copied
 
         def multiply(g, j):
             for u in range(PAIRS):
@@ -142,32 +159,27 @@ def tile_switchnet_fstar_pa_k_kernel(tc, x, k1, b1, grad_out, out):
                         stop=(g == GROUPS - 1 and u == PAIRS - 1 and e == 1),
                     )
 
-        weights(0, 0)
-        for quarter in range(QUARTERS):
-            rows = load_grad(0, quarter)
+        unswitched_next = undo_switch(load_grad(0))
+        for piece in range(PIECES):
+            unswitched = unswitched_next
+            if piece + 1 < PIECES:
+                unswitched_next = undo_switch(load_grad(piece + 1))
+            copied = transpose_grad(unswitched)
+            if piece < BLOCKS:
+                k_copied = transpose_weights(load_weights(piece))
+            if piece == QUARTERS:
+                for j in range(BLOCKS):
+                    multiply(0, j)
             for j in range(BLOCKS):
-                grad_block(rows, quarter, j, 2 * j)
-        for j in range(1, BLOCKS):
-            weights(j, 0)
-            multiply(0, j - 1)
-        for quarter in range(QUARTERS - 1):
-            rows = load_grad(1, quarter)
-            for j in range(BLOCKS):
-                grad_block(rows, quarter, j, 2 * j)
-                if quarter == 0 and j == 1:
-                    multiply(0, BLOCKS - 1)
-        rows = load_grad(1, QUARTERS - 1)
-        for j in range(BLOCKS):
-            grad_block(rows, QUARTERS - 1, j, 2 * j)
-            if j >= 2:
-                multiply(1, j - 2)
-        quantise_held()
-        multiply(1, BLOCKS - 2)
-        multiply(1, BLOCKS - 1)
+                quantise_grad(piece, j, copied)
+                if piece == PIECES - 1:
+                    multiply(1, j)
+            if piece < BLOCKS:
+                quantise_weights(piece, k_copied)
 
         gh = [keep.tile([P, SAMPLES], F32, name="gh%d" % j) for j in range(BLOCKS)]
         for j in range(BLOCKS):
-            empty_bank(j)(
+            (nc.vector.tensor_copy if j % 2 == 0 else nc.scalar.copy)(
                 out=gh[j][:].rearrange("k (q s) -> k q s", q=QUARTERS),
                 in_=acc[j][:].rearrange("k (q h s) -> k q h s", q=QUARTERS, h=2, s=QUARTER)[:, :, 0, :],
             )
@@ -177,7 +189,7 @@ def tile_switchnet_fstar_pa_k_kernel(tc, x, k1, b1, grad_out, out):
                 nc.tensor.transpose(bank[:, j * P : (j + 1) * P], gh[j][:, half * P : (half + 1) * P], ident[:])
             grid = result_pool.tile([P, BANK], F32, name="grid")
             for br in range(2):
-                empty_bank(half)(
+                (nc.vector.tensor_copy if half == 0 else nc.scalar.copy)(
                     out=grid[:, br * 256 : (br + 1) * 256].rearrange("b (r c x) -> b r c x", r=8, c=2, x=16),
                     in_=bank[:, br * 256 : (br + 1) * 256].rearrange("b (c r x) -> b r c x", c=2, r=8, x=16),
                 )

@@ -28,6 +28,7 @@ QUARTERS = SAMPLES // QUARTER
 PIECES = GROUPS * QUARTERS
 HALF_R = K_PASS // 2
 SWITCHED = BLOCKS * PLANES
+BY_VECTOR = 3
 SORT = 4
 FILLER = QUARTER
 GY_COLS = SAMPLES * 2 + FILLER
@@ -80,8 +81,8 @@ def tile_switchnet_fstar_pa_k_kernel(tc, x, k1, b1, grad_out, out):
 
         def undo_switch(rows):
             by_r = rows[:].rearrange("q (r c) -> q r c", c=SWITCHED)
-            unswitched = sorted_pool.tile([P, SWITCHED, HALF_R], BF16, name="unswitched")
-            for c in range(0, SWITCHED, SORT):
+            unswitched = sorted_pool.tile([P, BY_VECTOR * PLANES, HALF_R], BF16, name="unswitched")
+            for c in range(0, BY_VECTOR * PLANES, SORT):
                 nc.vector.tensor_copy(
                     out=unswitched[:, c : c + SORT, :].rearrange("q c r -> q r c"), in_=by_r[:, :, c : c + SORT]
                 )
@@ -90,12 +91,33 @@ def tile_switchnet_fstar_pa_k_kernel(tc, x, k1, b1, grad_out, out):
         def transpose_grad(unswitched):
             words = unswitched[:].bitcast(F32)
             copied = []
-            for c in range(0, SWITCHED, 4):
+            for c in range(0, BY_VECTOR * PLANES, 4):
                 bank = banks.tile([P, BANK], F32, name="bank")
                 for i in range(4):
                     nc.tensor.transpose(bank[:, i * P : (i + 1) * P], words[:, c + i, :], ident[:])
                 grouped = stage.tile([P, 2 * BANK], BF16, name="gy_grouped", align_bytes=64)
                 nc.scalar.copy(out=grouped[:].bitcast(F32), in_=bank[:])
+                copied.append(grouped)
+            return copied
+
+        def transpose_switched(rows, j):
+            words = rows[:].bitcast(F32).rearrange("q (p w) -> q p w", w=SWITCHED)
+            copied = []
+            for i in range(2):
+                bank = banks.tile([P, BANK], F32, name="bank")
+                for uu in range(2):
+                    for odd in range(2):
+                        nc.tensor.transpose(
+                            bank[:, (2 * uu + odd) * P : (2 * uu + odd + 1) * P],
+                            words[:, :, odd * (SWITCHED // 2) + j * PAIRS + 2 * i + uu],
+                            ident[:],
+                        )
+                grouped = stage.tile([P, 2 * BANK], BF16, name="gy_grouped", align_bytes=64)
+                for uu in range(2):
+                    nc.scalar.copy(
+                        out=grouped[:, uu * BANK : (uu + 1) * BANK].rearrange("p (e q o) -> p e q o", e=2, q=P, o=2),
+                        in_=bank[:, uu * 2 * P : (uu + 1) * 2 * P].bitcast(BF16).rearrange("p (o q e) -> p e q o", o=2, q=P, e=2),
+                    )
                 copied.append(grouped)
             return copied
 
@@ -159,12 +181,17 @@ def tile_switchnet_fstar_pa_k_kernel(tc, x, k1, b1, grad_out, out):
                         stop=(g == GROUPS - 1 and u == PAIRS - 1 and e == 1),
                     )
 
-        unswitched_next = undo_switch(load_grad(0))
+        rows_next = load_grad(0)
+        unswitched_next = undo_switch(rows_next)
         for piece in range(PIECES):
+            rows = rows_next
             unswitched = unswitched_next
             if piece + 1 < PIECES:
-                unswitched_next = undo_switch(load_grad(piece + 1))
+                rows_next = load_grad(piece + 1)
+                unswitched_next = undo_switch(rows_next)
             copied = transpose_grad(unswitched)
+            for j in range(BY_VECTOR, BLOCKS):
+                copied.extend(transpose_switched(rows, j))
             if piece < BLOCKS:
                 k_copied = transpose_weights(load_weights(piece))
             if piece == QUARTERS:

@@ -28,8 +28,7 @@ QUARTERS = SAMPLES // QUARTER
 PIECES = GROUPS * QUARTERS
 HALF_R = K_PASS // 2
 SWITCHED = BLOCKS * PLANES
-BY_VECTOR = 3
-SORT = 4
+RUN = 4
 FILLER = QUARTER
 GY_COLS = SAMPLES * 2 + FILLER
 
@@ -79,45 +78,27 @@ def tile_switchnet_fstar_pa_k_kernel(tc, x, k1, b1, grad_out, out):
                 )
             return rows
 
-        def undo_switch(rows):
-            by_r = rows[:].rearrange("q (r c) -> q r c", c=SWITCHED)
-            unswitched = sorted_pool.tile([P, BY_VECTOR * PLANES, HALF_R], BF16, name="unswitched")
-            for c in range(0, BY_VECTOR * PLANES, SORT):
+        def pair_up(rows):
+            by_r = rows[:].rearrange("q (rp o c) -> q rp o c", o=2, c=SWITCHED)
+            paired = sorted_pool.tile([P, HALF_R * SWITCHED], BF16, name="paired")
+            by_pair = paired[:].rearrange("q (rp c o) -> q rp c o", c=SWITCHED, o=2)
+            for j in range(BLOCKS):
+                cols = slice(j * PLANES, (j + 1) * PLANES)
                 nc.vector.tensor_copy(
-                    out=unswitched[:, c : c + SORT, :].rearrange("q c r -> q r c"), in_=by_r[:, :, c : c + SORT]
+                    out=by_pair[:, :, cols, :].rearrange("q rp (cg i) o -> q rp cg o i", i=RUN),
+                    in_=by_r[:, :, :, cols].rearrange("q rp o (cg i) -> q rp cg o i", i=RUN),
                 )
-            return unswitched
+            return paired
 
-        def transpose_grad(unswitched):
-            words = unswitched[:].bitcast(F32)
+        def transpose_grad(paired):
+            words = paired[:].bitcast(F32).rearrange("q (rp c) -> q rp c", c=SWITCHED)
             copied = []
-            for c in range(0, BY_VECTOR * PLANES, 4):
+            for c in range(0, SWITCHED, 4):
                 bank = banks.tile([P, BANK], F32, name="bank")
                 for i in range(4):
-                    nc.tensor.transpose(bank[:, i * P : (i + 1) * P], words[:, c + i, :], ident[:])
+                    nc.tensor.transpose(bank[:, i * P : (i + 1) * P], words[:, :, c + i], ident[:])
                 grouped = stage.tile([P, 2 * BANK], BF16, name="gy_grouped", align_bytes=64)
                 nc.scalar.copy(out=grouped[:].bitcast(F32), in_=bank[:])
-                copied.append(grouped)
-            return copied
-
-        def transpose_switched(rows, j):
-            words = rows[:].bitcast(F32).rearrange("q (p w) -> q p w", w=SWITCHED)
-            copied = []
-            for i in range(2):
-                bank = banks.tile([P, BANK], F32, name="bank")
-                for uu in range(2):
-                    for odd in range(2):
-                        nc.tensor.transpose(
-                            bank[:, (2 * uu + odd) * P : (2 * uu + odd + 1) * P],
-                            words[:, :, odd * (SWITCHED // 2) + j * PAIRS + 2 * i + uu],
-                            ident[:],
-                        )
-                grouped = stage.tile([P, 2 * BANK], BF16, name="gy_grouped", align_bytes=64)
-                for uu in range(2):
-                    nc.scalar.copy(
-                        out=grouped[:, uu * BANK : (uu + 1) * BANK].rearrange("p (e q o) -> p e q o", e=2, q=P, o=2),
-                        in_=bank[:, uu * 2 * P : (uu + 1) * 2 * P].bitcast(BF16).rearrange("p (o q e) -> p e q o", o=2, q=P, e=2),
-                    )
                 copied.append(grouped)
             return copied
 
@@ -181,17 +162,12 @@ def tile_switchnet_fstar_pa_k_kernel(tc, x, k1, b1, grad_out, out):
                         stop=(g == GROUPS - 1 and u == PAIRS - 1 and e == 1),
                     )
 
-        rows_next = load_grad(0)
-        unswitched_next = undo_switch(rows_next)
+        paired_next = pair_up(load_grad(0))
         for piece in range(PIECES):
-            rows = rows_next
-            unswitched = unswitched_next
+            paired = paired_next
             if piece + 1 < PIECES:
-                rows_next = load_grad(piece + 1)
-                unswitched_next = undo_switch(rows_next)
-            copied = transpose_grad(unswitched)
-            for j in range(BY_VECTOR, BLOCKS):
-                copied.extend(transpose_switched(rows, j))
+                paired_next = pair_up(load_grad(piece + 1))
+            copied = transpose_grad(paired)
             if piece < BLOCKS:
                 k_copied = transpose_weights(load_weights(piece))
             if piece == QUARTERS:

@@ -78,40 +78,45 @@ def tile_switchnet_fstar_pa_k_kernel(tc, x, k1, b1, grad_out, out):
                 )
             return rows
 
-        def pair_up(rows):
-            by_r = rows[:].rearrange("q (rp o c) -> q rp o c", o=2, c=SWITCHED)
-            paired = sorted_pool.tile([P, HALF_R * SWITCHED], BF16, name="paired")
-            by_pair = paired[:].rearrange("q (rp c o) -> q rp c o", c=SWITCHED, o=2)
-            for j in range(BLOCKS):
-                cols = slice(j * PLANES, (j + 1) * PLANES)
+        def slices_of(step):
+            if step < PIECES - 2:
+                return [(step, j) for j in range(BLOCKS)]
+            return [(piece, step - (PIECES - 2)) for piece in (PIECES - 2, PIECES - 1)]
+
+        def pair_up(step):
+            paired = sorted_pool.tile([P, len(slices_of(step)) * HALF_R * PLANES], BF16, name="paired")
+            for k, (piece, j) in enumerate(slices_of(step)):
                 nc.vector.tensor_copy(
-                    out=by_pair[:, :, cols, :].rearrange("q rp (cg i) o -> q rp cg o i", i=RUN),
-                    in_=by_r[:, :, :, cols].rearrange("q rp o (cg i) -> q rp cg o i", i=RUN),
+                    out=paired[:, k * HALF_R * PLANES : (k + 1) * HALF_R * PLANES].rearrange(
+                        "q (rp cg i o) -> q rp cg o i", cg=PLANES // RUN, i=RUN, o=2
+                    ),
+                    in_=rows_of[piece][:]
+                    .rearrange("q (rp o c) -> q rp o c", o=2, c=SWITCHED)[:, :, :, j * PLANES : (j + 1) * PLANES]
+                    .rearrange("q rp o (cg i) -> q rp cg o i", i=RUN),
                 )
             return paired
 
         def transpose_grad(paired):
-            words = paired[:].bitcast(F32).rearrange("q (rp c) -> q rp c", c=SWITCHED)
+            words = paired[:].bitcast(F32).rearrange("q (k rp m) -> q k m rp", rp=HALF_R // 2, m=PLANES)
             copied = []
-            for c in range(0, SWITCHED, 4):
+            for n in range(2 * words.shape[1]):
                 bank = banks.tile([P, BANK], F32, name="bank")
                 for i in range(4):
-                    nc.tensor.transpose(bank[:, i * P : (i + 1) * P], words[:, :, c + i], ident[:])
+                    nc.tensor.transpose(bank[:, i * P : (i + 1) * P], words[:, n // 2, 4 * (n % 2) + i, :], ident[:])
                 grouped = stage.tile([P, 2 * BANK], BF16, name="gy_grouped", align_bytes=64)
                 nc.scalar.copy(out=grouped[:].bitcast(F32), in_=bank[:])
                 copied.append(grouped)
             return copied
 
-        def quantise_grad(piece, j, copied):
+        def quantise_grad(piece, j, pair):
             quarter = piece % QUARTERS
             cols = slice(quarter * 2 * QUARTER, (quarter + 1) * 2 * QUARTER)
             for u in range(PAIRS):
-                grouped = copied[(j * PLANES + 2 * u) // 4]
                 first = (u % 2) * BANK
                 nc.vector.quantize_mx(
                     out=gy_codes[j][:, u, cols].bitcast(E5M2X4),
                     scales=gy_scales[j][:, u, cols],
-                    in_=grouped[:, first : first + BANK],
+                    in_=pair[u // 2][:, first : first + BANK],
                 )
 
         def load_weights(j):
@@ -162,23 +167,31 @@ def tile_switchnet_fstar_pa_k_kernel(tc, x, k1, b1, grad_out, out):
                         stop=(g == GROUPS - 1 and u == PAIRS - 1 and e == 1),
                     )
 
-        paired_next = pair_up(load_grad(0))
-        for piece in range(PIECES):
+        steps = PIECES - 2 + BLOCKS
+        rows_of = {}
+        rows_of[0] = load_grad(0)
+        paired_next = pair_up(0)
+        for step in range(steps):
             paired = paired_next
-            if piece + 1 < PIECES:
-                paired_next = pair_up(load_grad(piece + 1))
+            if step + 1 < PIECES - 1:
+                rows_of[step + 1] = load_grad(step + 1)
+            if step + 1 == PIECES - 2:
+                rows_of[PIECES - 1] = load_grad(PIECES - 1)
+            if step + 1 < steps:
+                paired_next = pair_up(step + 1)
             copied = transpose_grad(paired)
-            if piece < BLOCKS:
-                k_copied = transpose_weights(load_weights(piece))
-            if piece == QUARTERS:
+            if step < BLOCKS:
+                k_copied = transpose_weights(load_weights(step))
+            if step == QUARTERS:
                 for j in range(BLOCKS):
                     multiply(0, j)
-            for j in range(BLOCKS):
-                quantise_grad(piece, j, copied)
-                if piece == PIECES - 1:
-                    multiply(1, j)
-            if piece < BLOCKS:
-                quantise_weights(piece, k_copied)
+            if step > PIECES - 2:
+                multiply(1, step - (PIECES - 2) - 1)
+            for k, (piece, j) in enumerate(slices_of(step)):
+                quantise_grad(piece, j, copied[2 * k : 2 * k + 2])
+            if step < BLOCKS:
+                quantise_weights(step, k_copied)
+        multiply(1, BLOCKS - 1)
 
         gh = [keep.tile([P, SAMPLES], F32, name="gh%d" % j) for j in range(BLOCKS)]
         for j in range(BLOCKS):

@@ -59,7 +59,14 @@ def tile_switchnet_fstar_pa_k_kernel(tc, x, k1, b1, grad_out, out):
         k_scales = [keep.tile([P, 2 * PLANES * WINDOW], U8, name="k_scales%d" % j, align_bytes=64) for j in range(BLOCKS)]
         gy_codes = [keep.tile([P, PAIRS, GY_COLS], U32, name="gy_codes%d" % j, align_bytes=64) for j in range(BLOCKS)]
         gy_scales = [keep.tile([P, PAIRS, GY_COLS], U8, name="gy_scales%d" % j, align_bytes=64) for j in range(BLOCKS)]
-        acc = [sums.tile([P, N_PASS], F32, name="acc%d" % j) for j in range(BLOCKS)]
+        acc = []
+        turn_count = [0]
+
+        def next_bank():
+            turn_count[0] += 1
+            if acc or turn_count[0] % 2 == 0:
+                return banks.tile([P, BANK], F32, name="bank")
+            return sums.tile([P, BANK], F32, name="acc%d" % (turn_count[0] // 2 % BLOCKS))
 
         for j in range(BLOCKS):
             nc.vector.memset(gy_codes[j][:, :, 2 * SAMPLES :].bitcast(I32), 0)
@@ -100,7 +107,7 @@ def tile_switchnet_fstar_pa_k_kernel(tc, x, k1, b1, grad_out, out):
             words = paired[:].bitcast(F32).rearrange("q (k rp m) -> q k m rp", rp=HALF_R // 2, m=PLANES)
             copied = []
             for n in range(2 * words.shape[1]):
-                bank = banks.tile([P, BANK], F32, name="bank")
+                bank = next_bank()
                 for i in range(4):
                     nc.tensor.transpose(bank[:, i * P : (i + 1) * P], words[:, n // 2, 4 * (n % 2) + i, :], ident[:])
                 grouped = stage.tile([P, 2 * BANK], BF16, name="gy_grouped", align_bytes=64)
@@ -132,7 +139,7 @@ def tile_switchnet_fstar_pa_k_kernel(tc, x, k1, b1, grad_out, out):
             for raw in raws:
                 words = raw[:].bitcast(F32)
                 for i in range(4):
-                    bank = banks.tile([P, BANK], F32, name="bank")
+                    bank = next_bank()
                     for q in range(4):
                         nc.tensor.transpose(
                             bank[:, q * P : (q + 1) * P], words[:, i * BANK + q * P : i * BANK + (q + 1) * P], ident[:]
@@ -183,6 +190,8 @@ def tile_switchnet_fstar_pa_k_kernel(tc, x, k1, b1, grad_out, out):
             if step < BLOCKS:
                 k_copied = transpose_weights(load_weights(step))
             if step == QUARTERS:
+                for j in range(BLOCKS):
+                    acc.append(sums.tile([P, N_PASS], F32, name="acc%d" % j))
                 for j in range(BLOCKS):
                     multiply(0, j)
             if step > PIECES - 2:

from contextlib import ExitStack

import concourse.mybir as mybir
from concourse.masks import make_identity

F32 = mybir.dt.float32
BF16 = mybir.dt.bfloat16
I32 = mybir.dt.int32
U32 = mybir.dt.uint32
U8 = mybir.dt.uint8
E4M3X4 = mybir.dt.float8_e4m3fn_x4
E5M2X4 = mybir.dt.float8_e5m2_x4

P = 128
SAMPLES = 256
BLOCKS = 4
WINDOW = 128
PLANES = 8
R = 1024
K_PASS = 512
GROUPS = R // K_PASS
PAIRS = PLANES // 2
BANK = 512
N_PASS = 512

QUARTER = 64
QUARTERS = SAMPLES // QUARTER
PIECES = GROUPS * QUARTERS
HALF_R = K_PASS // 2
SWITCHED = BLOCKS * PLANES
RUN = 4
FILLER = QUARTER
GY_COLS = SAMPLES * 2 + FILLER

FLOPS = 2 * SAMPLES * BLOCKS * WINDOW * PLANES * R
BYTES = 2 * SAMPLES * BLOCKS * PLANES * R + 2 * BLOCKS * WINDOW * PLANES * R + 4 * SAMPLES * BLOCKS * WINDOW


def tile_switchnet_fstar_pa_k_kernel(tc, x, k1, b1, grad_out, out):
    nc = tc.nc
    flat_grad = grad_out.rearrange("b a c -> b (a c)")
    flat_out = out.rearrange("b g c -> b (g c)")

    with ExitStack() as ctx:
        keep = ctx.enter_context(tc.tile_pool(name="keep", bufs=1))
        grad_pool = ctx.enter_context(tc.tile_pool(name="grad", bufs=3))
        sorted_pool = ctx.enter_context(tc.tile_pool(name="sorted", bufs=2))
        weight_pool = ctx.enter_context(tc.tile_pool(name="weight", bufs=3))
        stage = ctx.enter_context(tc.tile_pool(name="stage", bufs=8))
        result_pool = ctx.enter_context(tc.tile_pool(name="result", bufs=2))
        sums = ctx.enter_context(tc.psum_pool(name="sums", bufs=1))
        banks = ctx.enter_context(tc.psum_pool(name="banks", bufs=4))
        ctx.enter_context(tc.manual_schedule())

        ident = keep.tile([P, P], F32, name="ident")
        make_identity(nc, ident[:])

        k_codes = [keep.tile([P, 2 * PLANES * WINDOW], U32, name="k_codes%d" % j, align_bytes=64) for j in range(BLOCKS)]
        k_scales = [keep.tile([P, 2 * PLANES * WINDOW], U8, name="k_scales%d" % j, align_bytes=64) for j in range(BLOCKS)]
        gy_codes = [keep.tile([P, PAIRS, GY_COLS], U32, name="gy_codes%d" % j, align_bytes=64) for j in range(BLOCKS)]
        gy_scales = [keep.tile([P, PAIRS, GY_COLS], U8, name="gy_scales%d" % j, align_bytes=64) for j in range(BLOCKS)]
        acc = []
        turn_count = [0]

        def next_bank():
            turn_count[0] += 1
            if acc or turn_count[0] % 2 == 0:
                return banks.tile([P, BANK], F32, name="bank")
            return sums.tile([P, BANK], F32, name="acc%d" % (turn_count[0] // 2 % BLOCKS))

        for j in range(BLOCKS):
            nc.vector.memset(gy_codes[j][:, :, 2 * SAMPLES :].bitcast(I32), 0)
            nc.vector.memset(gy_scales[j][:, :, 2 * SAMPLES :].bitcast(I32), 0)

        def load_grad(piece):
            g, quarter = divmod(piece, QUARTERS)
            rows = grad_pool.tile([P, HALF_R * SWITCHED], BF16, name="rows")
            for half in range(2):
                nc.sync.dma_start(
                    out=rows[half:P:2, :],
                    in_=flat_grad[
                        quarter * QUARTER : (quarter + 1) * QUARTER,
                        (2 * g + half) * HALF_R * SWITCHED : (2 * g + half + 1) * HALF_R * SWITCHED,
                    ],
                )
            return rows

        def slices_of(step):
            if step < PIECES - 2:
                return [(step, j) for j in range(BLOCKS)]
            return [(piece, step - (PIECES - 2)) for piece in (PIECES - 2, PIECES - 1)]

        def pair_up(step):
            paired = sorted_pool.tile([P, len(slices_of(step)) * HALF_R * PLANES], BF16, name="paired")
            for k, (piece, j) in enumerate(slices_of(step)):
                nc.vector.tensor_copy(
                    out=paired[:, k * HALF_R * PLANES : (k + 1) * HALF_R * PLANES].rearrange(
                        "q (rp cg i o) -> q rp cg o i", cg=PLANES // RUN, i=RUN, o=2
                    ),
                    in_=rows_of[piece][:]
                    .rearrange("q (rp o c) -> q rp o c", o=2, c=SWITCHED)[:, :, :, j * PLANES : (j + 1) * PLANES]
                    .rearrange("q rp o (cg i) -> q rp cg o i", i=RUN),
                )
            return paired

        def transpose_grad(paired):
            words = paired[:].bitcast(F32).rearrange("q (k rp m) -> q k m rp", rp=HALF_R // 2, m=PLANES)
            copied = []
            for n in range(2 * words.shape[1]):
                bank = next_bank()
                for i in range(4):
                    nc.tensor.transpose(bank[:, i * P : (i + 1) * P], words[:, n // 2, 4 * (n % 2) + i, :], ident[:])
                grouped = stage.tile([P, 2 * BANK], BF16, name="gy_grouped", align_bytes=64)
                nc.scalar.copy(out=grouped[:].bitcast(F32), in_=bank[:])
                copied.append(grouped)
            return copied

        def quantise_grad(piece, j, pair):
            quarter = piece % QUARTERS
            cols = slice(quarter * 2 * QUARTER, (quarter + 1) * 2 * QUARTER)
            for u in range(PAIRS):
                first = (u % 2) * BANK
                nc.vector.quantize_mx(
                    out=gy_codes[j][:, u, cols].bitcast(E5M2X4),
                    scales=gy_scales[j][:, u, cols],
                    in_=pair[u // 2][:, first : first + BANK],
                )

        def load_weights(j):
            raws = []
            for h in range(2):
                raw = weight_pool.tile([P, PLANES * R // 2], BF16, name="raw")
                nc.sync.dma_start(out=raw[:], in_=k1[j, :, h * (PLANES * R // 2) : (h + 1) * (PLANES * R // 2)])
                raws.append(raw)
            return raws

        def transpose_weights(raws):
            copied = []
            for raw in raws:
                words = raw[:].bitcast(F32)
                for i in range(4):
                    bank = next_bank()
                    for q in range(4):
                        nc.tensor.transpose(
                            bank[:, q * P : (q + 1) * P], words[:, i * BANK + q * P : i * BANK + (q + 1) * P], ident[:]
                        )
                    grouped = stage.tile([P, 2 * BANK], BF16, name="k_grouped", align_bytes=64)
                    nc.scalar.copy(
                        out=grouped[:].bitcast(F32).rearrange("p (c k u) -> p c k u", c=2, k=WINDOW, u=2),
                        in_=bank[:].rearrange("p (c u k) -> p c k u", c=2, u=2, k=WINDOW),
                    )
                    copied.append(grouped)
            return copied

        def quantise_weights(j, copied):
            for i in range(len(copied)):
                cols = slice(2 * i * WINDOW, (2 * i + 2) * WINDOW)
                nc.vector.quantize_mx(
                    out=k_codes[j][:, cols].bitcast(E4M3X4), scales=k_scales[j][:, cols], in_=copied[i][:]
                )

        def multiply(g, j):
            for u in range(PAIRS):
                for e in range(2):
                    k_cols = slice((2 * (2 * u + e) + g) * WINDOW, (2 * (2 * u + e) + g + 1) * WINDOW)
                    gy_cols = slice(e * QUARTER, e * QUARTER + N_PASS)
                    nc.tensor.matmul_mx(
                        out=acc[j][:],
                        lhsT=k_codes[j][:, k_cols].bitcast(E4M3X4),
                        lhsT_scale=k_scales[j][:, k_cols],
                        rhs=gy_codes[j][:, u, gy_cols].bitcast(E5M2X4),
                        rhs_scale=gy_scales[j][:, u, gy_cols],
                        start=(g == 0 and u == 0 and e == 0),
                        stop=(g == GROUPS - 1 and u == PAIRS - 1 and e == 1),
                    )

        steps = PIECES - 2 + BLOCKS
        rows_of = {}
        rows_of[0] = load_grad(0)
        paired_next = pair_up(0)
        for step in range(steps):
            paired = paired_next
            if step + 1 < PIECES - 1:
                rows_of[step + 1] = load_grad(step + 1)
            if step + 1 == PIECES - 2:
                rows_of[PIECES - 1] = load_grad(PIECES - 1)
            if step + 1 < steps:
                paired_next = pair_up(step + 1)
            copied = transpose_grad(paired)
            if step < BLOCKS:
                k_copied = transpose_weights(load_weights(step))
            if step == QUARTERS:
                for j in range(BLOCKS):
                    acc.append(sums.tile([P, N_PASS], F32, name="acc%d" % j))
                for j in range(BLOCKS):
                    multiply(0, j)
            if step > PIECES - 2:
                multiply(1, step - (PIECES - 2) - 1)
            for k, (piece, j) in enumerate(slices_of(step)):
                quantise_grad(piece, j, copied[2 * k : 2 * k + 2])
            if step < BLOCKS:
                quantise_weights(step, k_copied)
        multiply(1, BLOCKS - 1)

        gh = [keep.tile([P, SAMPLES], F32, name="gh%d" % j) for j in range(BLOCKS)]
        for j in range(BLOCKS):
            (nc.vector.tensor_copy if j % 2 == 0 else nc.scalar.copy)(
                out=gh[j][:].rearrange("k (q s) -> k q s", q=QUARTERS),
                in_=acc[j][:].rearrange("k (q h s) -> k q h s", q=QUARTERS, h=2, s=QUARTER)[:, :, 0, :],
            )
        for half in range(SAMPLES // P):
            bank = banks.tile([P, BANK], F32, name="bank")
            for j in range(BLOCKS):
                nc.tensor.transpose(bank[:, j * P : (j + 1) * P], gh[j][:, half * P : (half + 1) * P], ident[:])
            grid = result_pool.tile([P, BANK], F32, name="grid")
            for br in range(2):
                (nc.vector.tensor_copy if half == 0 else nc.scalar.copy)(
                    out=grid[:, br * 256 : (br + 1) * 256].rearrange("b (r c x) -> b r c x", r=8, c=2, x=16),
                    in_=bank[:, br * 256 : (br + 1) * 256].rearrange("b (c r x) -> b r c x", c=2, r=8, x=16),
                )
            nc.sync.dma_start(out=flat_out[half * P : (half + 1) * P, :], in_=grid[:])
